import numpy as np
import ml_dtypes


def mxq(x, axis, fmt="e4m3"):
    dtype, down = {"e4m3": (ml_dtypes.float8_e4m3fn, 7), "e5m2": (ml_dtypes.float8_e5m2, 14)}[fmt]
    v = np.moveaxis(np.asarray(x, np.float32).astype(ml_dtypes.bfloat16).astype(np.float64), axis, -1)
    blocks = v.reshape(v.shape[:-1] + (-1, 32))
    amax = np.abs(blocks).max(-1, keepdims=True)
    byte = np.maximum(np.where(amax > 0, np.frexp(amax)[1] - 1 + 127, 0) - down, 1)
    scale = np.exp2(byte - 127.0)
    codes = (blocks / scale).astype(np.float32).astype(dtype).astype(np.float64)
    return np.moveaxis((codes * scale).reshape(v.shape), -1, axis)


WIDE = False


def mx_kscale(k):
    if not WIDE:
        return np.ones(k)
    levels = np.array([10, -10, 5, -5, 0])
    a = np.random.permutation(np.resize(levels, k // 512 * 4)).reshape(k // 512, 4)
    idx = np.arange(k)
    return np.exp2(a[idx // 512, idx % 128 // 32])


BF16 = ml_dtypes.bfloat16


def bf(x):
    return np.asarray(x, np.float32).astype(BF16)


def f64(x):
    return np.asarray(x).astype(np.float64)


E2M1 = np.array([0.0, 0.5, 1.0, 1.5, 2.0, 3.0, 4.0, 6.0, -0.0, -0.5, -1.0, -1.5, -2.0, -3.0, -4.0, -6.0])


def pack_weight(w, fmt):
    k, n = w.shape
    w = f64(bf(w)).reshape(k // 32, 32, n)
    amax = np.abs(w).max(1)
    if fmt == "e4m3":
        byte = np.frexp(amax)[1] - 1 + 127 - 7
    else:
        mant, ex = np.frexp(amax / 6.0)
        byte = np.where(mant > 0.5, ex, ex - 1) + 127
    byte = np.clip(np.where(amax > 0, byte, 1), 1, 254)
    scaled = (w * np.exp2(127.0 - byte)[:, None, :]).reshape(k, n).astype(np.float32)
    by_word = np.ascontiguousarray(scaled.reshape(k // 512, 128, 4, n).transpose(0, 1, 3, 2))
    if fmt == "e4m3":
        words = by_word.astype(ml_dtypes.float8_e4m3fn).view(np.uint8)
    else:
        c = by_word.astype(ml_dtypes.float4_e2m1fn).view(np.uint8) & 0xF
        words = c[..., 0::2] | (c[..., 1::2] << 4)
    return np.ascontiguousarray(words), np.ascontiguousarray(byte.astype(np.uint8).reshape(k // 512, 16, n))


def unpack_weight(words, scales, fmt):
    g, p, n, _ = words.shape
    if fmt == "e4m3":
        vals = np.ascontiguousarray(words).view(ml_dtypes.float8_e4m3fn).astype(np.float64)
    else:
        nib = np.empty((g, p, n, 4), np.uint8)
        nib[..., 0::2] = words & 0xF
        nib[..., 1::2] = words >> 4
        vals = E2M1[nib]
    vals = vals * np.repeat(np.exp2(scales.astype(np.float64) - 127.0), 8, axis=1)[..., None]
    return vals.transpose(0, 1, 3, 2).reshape(g * 512, n)

def pack4(w):
    words, scales = pack_weight(w, "e2m1")
    return words.reshape(words.shape[0], 128, -1), scales


def unpack4(words, scales):
    return unpack_weight(words.reshape(words.shape[0], 128, -1, 2), scales, "e2m1")


B, F, D, L1, L2, L3 = 64, 8, 2, 256, 128, 4096
H2 = L2 // 2
K3 = H2 * F


def interact(h, x0):
    z = h.transpose(0, 2, 1)[:, :, :, None] * x0.transpose(0, 2, 1)[:, :, None, :]
    return z.reshape(z.shape[0], z.shape[1], -1)


def setup_inputs():
    a = mx_kscale(K3).reshape(H2, F)[:, 0]
    h2 = bf(np.maximum(np.random.standard_normal((B, H2, D)) * 0.75, 0.0) * a[None, :, None])
    x0 = bf(np.random.standard_normal((B, F, D)))
    W3_words, W3_scales = pack4(np.random.standard_normal((K3, L3)) / np.sqrt(K3) / np.repeat(a, F)[:, None])
    b3 = bf(np.random.standard_normal(L3) * 0.2)
    return {"h2": h2, "x0": x0, "W3_words": W3_words, "W3_scales": W3_scales, "b3": b3}


def reference(h2, x0, W3_words, W3_scales, b3):
    z = interact(f64(h2), f64(x0))
    y = np.maximum((mxq(z, 2, "e4m3") @ unpack4(W3_words, W3_scales)) + f64(b3), 0.0)
    return y.transpose(0, 2, 1).sum(axis=2)

@@ -1,0 +1,154 @@
+from contextlib import ExitStack
+
+import concourse.mybir as mybir
+from concourse.masks import make_identity
+
+BF16 = mybir.dt.bfloat16
+F32 = mybir.dt.float32
+I32 = mybir.dt.int32
+U8 = mybir.dt.uint8
+U32 = mybir.dt.uint32
+FP8X4 = mybir.dt.float8_e4m3fn_x4
+FP4X4 = mybir.dt.float4_e2m1fn_x4
+ALU = mybir.AluOpType
+ACT = mybir.ActivationFunctionType
+
+P = 128
+PACK = 4
+B, F_HID, F_RAW, D = 64, 64, 8, 2
+C = 4096
+ROWS = D * B
+C_TILE = 128
+BANK_TILES = 4
+HALVES = 2
+GROUPS = C // (HALVES * BANK_TILES * C_TILE)
+HALF_TILES = GROUPS * BANK_TILES
+GROUP_COLS = BANK_TILES * C_TILE
+
+FLOPS = 2 * ROWS * F_HID * F_RAW * C
+
+
+def tile_cin_pb_s_kernel(tc, h2, x0, W3_words, W3_scales, b3, out):
+    nc = tc.nc
+    with ExitStack() as ctx:
+        keep = ctx.enter_context(tc.tile_pool(name="keep", bufs=1))
+        work = ctx.enter_context(tc.tile_pool(name="work", bufs=3))
+        acc_pool = ctx.enter_context(tc.psum_pool(name="acc", bufs=3))
+        turned_pool = ctx.enter_context(tc.psum_pool(name="turned", bufs=2))
+
+        h2_rows = h2.rearrange("b f d -> b (f d)")
+        x0_rows = x0.rearrange("b j d -> b (j d)")
+        x0_sb = keep.tile([P, F_RAW * D], BF16)
+        h2_sb = keep.tile([P, F_HID * D], BF16)
+        nc.sync.dma_start(out=x0_sb[0:B, :], in_=x0_rows)
+        nc.sync.dma_start(out=x0_sb[B:P, 0 : F_RAW * D - 1], in_=x0_rows[:, 1:])
+        nc.sync.dma_start(out=h2_sb[0:B, :], in_=h2_rows)
+        nc.sync.dma_start(out=h2_sb[B:P, 0 : F_HID * D - 1], in_=h2_rows[:, 1:])
+
+        w_scales = keep.tile([P, C], U8, align_bytes=64)
+        nc.vector.memset(w_scales[:].bitcast(I32), 0)
+        for quad in range(4):
+            nc.sync.dma_start(
+                out=w_scales[32 * quad : 32 * quad + 4, :].bitcast(I32),
+                in_=W3_scales[0, 4 * quad : 4 * quad + 4, :].bitcast(I32),
+            )
+
+        b3_rows = keep.tile([P, P], BF16)
+        nc.gpsimd.memset(b3_rows[:], 0.0)
+        nc.scalar.dma_start(
+            out=b3_rows[0 : C // C_TILE, :], in_=b3.rearrange("(t c) -> t c", c=C_TILE)
+        )
+
+        w_words = keep.tile([P, 2 * C], U8, align_bytes=64)
+        words_dram = W3_words[0].rearrange("p (h g n) -> p h g n", h=HALVES, g=GROUPS)
+        words_sbuf = w_words[:].rearrange("p (h g n) -> p h g n", h=HALVES, g=GROUPS)
+        for g in range(GROUPS):
+            nc.sync.dma_start(
+                out=words_sbuf[:, :, g, :].bitcast(I32), in_=words_dram[:, :, g, :].bitcast(I32)
+            )
+
+        ident_bf16 = keep.tile([P, P], BF16)
+        make_identity(nc, ident_bf16[:])
+        ident_f32 = keep.tile([P, P], F32)
+        make_identity(nc, ident_f32[:])
+
+        h2_field = h2_sb[:].rearrange("r (f d) -> r f d", d=D)[:, :, 0]
+        x0_field = x0_sb[:].rearrange("r (j d) -> r j d", d=D)[:, :, 0]
+        z_shape = [P, PACK, F_HID, F_RAW // PACK]
+        z_rows = keep.tile(z_shape, BF16)
+        nc.vector.tensor_tensor(
+            out=z_rows[:],
+            in0=h2_field.unsqueeze(1).unsqueeze(3).to_broadcast(z_shape),
+            in1=x0_field.rearrange("r (s t) -> r t s", t=PACK).unsqueeze(2).to_broadcast(z_shape),
+            op=ALU.mult,
+        )
+        z_turned = turned_pool.tile([P, PACK, ROWS], BF16, tag="turned")
+        for t in range(PACK):
+            nc.tensor.transpose(
+                z_turned[:, t, :], z_rows[:, t, :, :].rearrange("r f s -> r (f s)"), ident_bf16[:]
+            )
+        b3_turned = turned_pool.tile([P, P], BF16, tag="turned")
+        nc.tensor.transpose(b3_turned[:], b3_rows[:], ident_bf16[:])
+
+        z_grouped = keep.tile([P, ROWS, PACK], BF16, align_bytes=64)
+        nc.vector.tensor_copy(out=z_grouped[:], in_=z_turned[:].rearrange("p t r -> p r t"))
+        z_codes = keep.tile([P, ROWS], U32, align_bytes=64)
+        z_scales = keep.tile([P, ROWS], U8, align_bytes=64)
+        nc.vector.quantize_mx(
+            out=z_codes[:].bitcast(FP8X4),
+            scales=z_scales[:],
+            in_=z_grouped[:].rearrange("p r t -> p (r t)"),
+        )
+
+        bias = keep.tile([P, C // C_TILE], F32)
+        nc.scalar.copy(out=bias[:], in_=b3_turned[:, 0 : C // C_TILE])
+
+        out_rows = out.rearrange("b (h n) -> (b h) n", h=HALVES)
+        out_sb = keep.tile([P, C // HALVES], F32)
+
+        for g in range(GROUPS):
+            y = work.tile([P, HALVES, BANK_TILES, ROWS], F32)
+            for h in range(HALVES):
+                acc = acc_pool.tile([P, BANK_TILES, ROWS], F32, tag="acc%d" % h)
+                first = h * HALF_TILES + g * BANK_TILES
+                for i in range(BANK_TILES):
+                    c0 = (first + i) * C_TILE
+                    nc.tensor.matmul_mx(
+                        out=acc[:, i, :],
+                        lhsT=w_words[:, 2 * c0 : 2 * (c0 + C_TILE)].bitcast(FP4X4),
+                        lhsT_scale=w_scales[:, c0 : c0 + C_TILE],
+                        rhs=z_codes[:].bitcast(FP8X4),
+                        rhs_scale=z_scales[:],
+                        start=True,
+                        stop=True,
+                    )
+                for i in range(BANK_TILES):
+                    tile_bias = bias[:, first + i : first + i + 1]
+                    if h == 0:
+                        nc.scalar.activation(
+                            out=y[:, h, i, :], in_=acc[:, i, :], func=ACT.Relu, bias=tile_bias, scale=1.0
+                        )
+                    else:
+                        nc.vector.tensor_scalar(
+                            out=y[:, h, i, :],
+                            in0=acc[:, i, :],
+                            scalar1=tile_bias,
+                            scalar2=0.0,
+                            op0=ALU.add,
+                            op1=ALU.max,
+                        )
+
+            y_by_d = y[:].rearrange("c h i (d b) -> c d i b h", d=D)
+            y_sum = work.tile([P, BANK_TILES, B, HALVES], F32)
+            nc.vector.tensor_tensor(
+                out=y_sum[:], in0=y_by_d[:, 0, :, :, :], in1=y_by_d[:, 1, :, :, :], op=ALU.add
+            )
+
+            y_turned = turned_pool.tile([P, BANK_TILES, C_TILE], F32, tag="turned")
+            for i in range(BANK_TILES):
+                nc.tensor.transpose(
+                    y_turned[:, i, :], y_sum[:, i, :, :].rearrange("c b h -> c (b h)"), ident_f32[:]
+                )
+            cols = slice(g * GROUP_COLS, (g + 1) * GROUP_COLS)
+            nc.scalar.copy(out=out_sb[:, cols], in_=y_turned[:].rearrange("r i c -> r (i c)"))
+            nc.sync.dma_start(out=out_rows[:, cols], in_=out_sb[:, cols])

@@ -24,6 +24,8 @@ HALVES = 2
 GROUPS = C // (HALVES * BANK_TILES * C_TILE)
 HALF_TILES = GROUPS * BANK_TILES
 GROUP_COLS = BANK_TILES * C_TILE
+ACC_ROUNDS = 3
+RELU_AHEAD = 2
 
 FLOPS = 2 * ROWS * F_HID * F_RAW * C
 
@@ -33,8 +35,9 @@ def tile_cin_pb_s_kernel(tc, h2, x0, W3_words, W3_scales, b3, out):
     with ExitStack() as ctx:
         keep = ctx.enter_context(tc.tile_pool(name="keep", bufs=1))
         work = ctx.enter_context(tc.tile_pool(name="work", bufs=3))
-        acc_pool = ctx.enter_context(tc.psum_pool(name="acc", bufs=3))
+        acc_pool = ctx.enter_context(tc.psum_pool(name="acc", bufs=ACC_ROUNDS))
         turned_pool = ctx.enter_context(tc.psum_pool(name="turned", bufs=2))
+        ctx.enter_context(tc.manual_schedule())
 
         h2_rows = h2.rearrange("b f d -> b (f d)")
         x0_rows = x0.rearrange("b j d -> b (j d)")
@@ -106,15 +109,21 @@ def tile_cin_pb_s_kernel(tc, h2, x0, W3_words, W3_scales, b3, out):
         out_rows = out.rearrange("b (h n) -> (b h) n", h=HALVES)
         out_sb = keep.tile([P, C // HALVES], F32)
 
-        for g in range(GROUPS):
-            y = work.tile([P, HALVES, BANK_TILES, ROWS], F32)
+        acc = {}
+        y = {}
+        y_sum = {}
+        y_turned = {}
+
+        def first_tile(g, h):
+            return h * HALF_TILES + g * BANK_TILES
+
+        def passes(g):
             for h in range(HALVES):
-                acc = acc_pool.tile([P, BANK_TILES, ROWS], F32, tag="acc%d" % h)
-                first = h * HALF_TILES + g * BANK_TILES
+                acc[g, h] = acc_pool.tile([P, BANK_TILES, ROWS], F32, name="acc%d" % h)
                 for i in range(BANK_TILES):
-                    c0 = (first + i) * C_TILE
+                    c0 = (first_tile(g, h) + i) * C_TILE
                     nc.tensor.matmul_mx(
-                        out=acc[:, i, :],
+                        out=acc[g, h][:, i, :],
                         lhsT=w_words[:, 2 * c0 : 2 * (c0 + C_TILE)].bitcast(FP4X4),
                         lhsT_scale=w_scales[:, c0 : c0 + C_TILE],
                         rhs=z_codes[:].bitcast(FP8X4),
@@ -122,33 +131,58 @@ def tile_cin_pb_s_kernel(tc, h2, x0, W3_words, W3_scales, b3, out):
                         start=True,
                         stop=True,
                     )
-                for i in range(BANK_TILES):
-                    tile_bias = bias[:, first + i : first + i + 1]
-                    if h == 0:
-                        nc.scalar.activation(
-                            out=y[:, h, i, :], in_=acc[:, i, :], func=ACT.Relu, bias=tile_bias, scale=1.0
-                        )
-                    else:
-                        nc.vector.tensor_scalar(
-                            out=y[:, h, i, :],
-                            in0=acc[:, i, :],
-                            scalar1=tile_bias,
-                            scalar2=0.0,
-                            op0=ALU.add,
-                            op1=ALU.max,
-                        )
 
-            y_by_d = y[:].rearrange("c h i (d b) -> c d i b h", d=D)
-            y_sum = work.tile([P, BANK_TILES, B, HALVES], F32)
+        def bias_relu(g):
+            y[g] = work.tile([P, HALVES, BANK_TILES, ROWS], F32, name="y")
+            for i in range(BANK_TILES):
+                t_left = first_tile(g, 0) + i
+                nc.vector.tensor_scalar(
+                    out=y[g][:, 0, i, :],
+                    in0=acc[g, 0][:, i, :],
+                    scalar1=bias[:, t_left : t_left + 1],
+                    scalar2=0.0,
+                    op0=ALU.add,
+                    op1=ALU.max,
+                )
+            for i in range(BANK_TILES):
+                t_right = first_tile(g, 1) + i
+                nc.scalar.activation(
+                    out=y[g][:, 1, i, :],
+                    in_=acc[g, 1][:, i, :],
+                    func=ACT.Relu,
+                    bias=bias[:, t_right : t_right + 1],
+                    scale=1.0,
+                )
+
+        def sum_over_d(g):
+            y_by_d = y[g][:].rearrange("c h i (d b) -> c d i b h", d=D)
+            y_sum[g] = work.tile([P, BANK_TILES, B, HALVES], F32, name="y_sum")
             nc.vector.tensor_tensor(
-                out=y_sum[:], in0=y_by_d[:, 0, :, :, :], in1=y_by_d[:, 1, :, :, :], op=ALU.add
+                out=y_sum[g][:], in0=y_by_d[:, 0, :, :, :], in1=y_by_d[:, 1, :, :, :], op=ALU.add
             )
 
-            y_turned = turned_pool.tile([P, BANK_TILES, C_TILE], F32, tag="turned")
+        def turn_back(g):
+            y_turned[g] = turned_pool.tile([P, BANK_TILES, C_TILE], F32, name="y_turned", tag="turned")
             for i in range(BANK_TILES):
                 nc.tensor.transpose(
-                    y_turned[:, i, :], y_sum[:, i, :, :].rearrange("c b h -> c (b h)"), ident_f32[:]
+                    y_turned[g][:, i, :],
+                    y_sum[g][:, i, :, :].rearrange("c b h -> c (b h)"),
+                    ident_f32[:],
                 )
+
+        def copy_and_store(g):
             cols = slice(g * GROUP_COLS, (g + 1) * GROUP_COLS)
-            nc.scalar.copy(out=out_sb[:, cols], in_=y_turned[:].rearrange("r i c -> r (i c)"))
+            nc.scalar.copy(out=out_sb[:, cols], in_=y_turned[g][:].rearrange("r i c -> r (i c)"))
             nc.sync.dma_start(out=out_rows[:, cols], in_=out_sb[:, cols])
+
+        for g in range(GROUPS):
+            passes(g)
+        for g in range(RELU_AHEAD):
+            bias_relu(g)
+        for g in range(GROUPS):
+            sum_over_d(g)
+            if g + RELU_AHEAD < GROUPS:
+                bias_relu(g + RELU_AHEAD)
+            turn_back(g)
+        for g in range(GROUPS):
+            copy_and_store(g)

@@ -21,9 +21,9 @@ ROWS = D * B
 C_TILE = 128
 BANK_TILES = 4
 HALVES = 2
-GROUPS = C // (HALVES * BANK_TILES * C_TILE)
-HALF_TILES = GROUPS * BANK_TILES
-GROUP_COLS = BANK_TILES * C_TILE
+HALF_TILES = C // (HALVES * C_TILE)
+W_LOADS = 4
+LAST_TILES = 2
 ACC_ROUNDS = 3
 RELU_AHEAD = 2
 
@@ -63,9 +63,9 @@ def tile_cin_pb_s_kernel(tc, h2, x0, W3_words, W3_scales, b3, out):
         )
 
         w_words = keep.tile([P, 2 * C], U8, align_bytes=64)
-        words_dram = W3_words[0].rearrange("p (h g n) -> p h g n", h=HALVES, g=GROUPS)
-        words_sbuf = w_words[:].rearrange("p (h g n) -> p h g n", h=HALVES, g=GROUPS)
-        for g in range(GROUPS):
+        words_dram = W3_words[0].rearrange("p (h g n) -> p h g n", h=HALVES, g=W_LOADS)
+        words_sbuf = w_words[:].rearrange("p (h g n) -> p h g n", h=HALVES, g=W_LOADS)
+        for g in range(W_LOADS):
             nc.sync.dma_start(
                 out=words_sbuf[:, :, g, :].bitcast(I32), in_=words_dram[:, :, g, :].bitcast(I32)
             )
@@ -109,21 +109,22 @@ def tile_cin_pb_s_kernel(tc, h2, x0, W3_words, W3_scales, b3, out):
         out_rows = out.rearrange("b (h n) -> (b h) n", h=HALVES)
         out_sb = keep.tile([P, C // HALVES], F32)
 
+        rounds = [(first, BANK_TILES) for first in range(0, HALF_TILES - BANK_TILES, BANK_TILES)]
+        rounds += [(first, LAST_TILES) for first in range(HALF_TILES - BANK_TILES, HALF_TILES, LAST_TILES)]
+
         acc = {}
         y = {}
         y_sum = {}
         y_turned = {}
 
-        def first_tile(g, h):
-            return h * HALF_TILES + g * BANK_TILES
-
-        def passes(g):
+        def passes(n):
+            first, tiles = rounds[n]
             for h in range(HALVES):
-                acc[g, h] = acc_pool.tile([P, BANK_TILES, ROWS], F32, name="acc%d" % h)
-                for i in range(BANK_TILES):
-                    c0 = (first_tile(g, h) + i) * C_TILE
+                acc[n, h] = acc_pool.tile([P, tiles, ROWS], F32, name="acc%d" % h)
+                for i in range(tiles):
+                    c0 = (h * HALF_TILES + first + i) * C_TILE
                     nc.tensor.matmul_mx(
-                        out=acc[g, h][:, i, :],
+                        out=acc[n, h][:, i, :],
                         lhsT=w_words[:, 2 * c0 : 2 * (c0 + C_TILE)].bitcast(FP4X4),
                         lhsT_scale=w_scales[:, c0 : c0 + C_TILE],
                         rhs=z_codes[:].bitcast(FP8X4),
@@ -132,57 +133,61 @@ def tile_cin_pb_s_kernel(tc, h2, x0, W3_words, W3_scales, b3, out):
                         stop=True,
                     )
 
-        def bias_relu(g):
-            y[g] = work.tile([P, HALVES, BANK_TILES, ROWS], F32, name="y")
-            for i in range(BANK_TILES):
-                t_left = first_tile(g, 0) + i
+        def bias_relu(n):
+            first, tiles = rounds[n]
+            y[n] = work.tile([P, HALVES, tiles, ROWS], F32, name="y")
+            for i in range(tiles):
+                t_left = first + i
                 nc.vector.tensor_scalar(
-                    out=y[g][:, 0, i, :],
-                    in0=acc[g, 0][:, i, :],
+                    out=y[n][:, 0, i, :],
+                    in0=acc[n, 0][:, i, :],
                     scalar1=bias[:, t_left : t_left + 1],
                     scalar2=0.0,
                     op0=ALU.add,
                     op1=ALU.max,
                 )
-            for i in range(BANK_TILES):
-                t_right = first_tile(g, 1) + i
+            for i in range(tiles):
+                t_right = HALF_TILES + first + i
                 nc.scalar.activation(
-                    out=y[g][:, 1, i, :],
-                    in_=acc[g, 1][:, i, :],
+                    out=y[n][:, 1, i, :],
+                    in_=acc[n, 1][:, i, :],
                     func=ACT.Relu,
                     bias=bias[:, t_right : t_right + 1],
                     scale=1.0,
                 )
 
-        def sum_over_d(g):
-            y_by_d = y[g][:].rearrange("c h i (d b) -> c d i b h", d=D)
-            y_sum[g] = work.tile([P, BANK_TILES, B, HALVES], F32, name="y_sum")
+        def sum_over_d(n):
+            tiles = rounds[n][1]
+            y_by_d = y[n][:].rearrange("c h i (d b) -> c d i b h", d=D)
+            y_sum[n] = work.tile([P, tiles, B, HALVES], F32, name="y_sum")
             nc.vector.tensor_tensor(
-                out=y_sum[g][:], in0=y_by_d[:, 0, :, :, :], in1=y_by_d[:, 1, :, :, :], op=ALU.add
+                out=y_sum[n][:], in0=y_by_d[:, 0, :, :, :], in1=y_by_d[:, 1, :, :, :], op=ALU.add
             )
 
-        def turn_back(g):
-            y_turned[g] = turned_pool.tile([P, BANK_TILES, C_TILE], F32, name="y_turned", tag="turned")
-            for i in range(BANK_TILES):
+        def turn_back(n):
+            tiles = rounds[n][1]
+            y_turned[n] = turned_pool.tile([P, tiles, C_TILE], F32, name="y_turned", tag="turned")
+            for i in range(tiles):
                 nc.tensor.transpose(
-                    y_turned[g][:, i, :],
-                    y_sum[g][:, i, :, :].rearrange("c b h -> c (b h)"),
+                    y_turned[n][:, i, :],
+                    y_sum[n][:, i, :, :].rearrange("c b h -> c (b h)"),
                     ident_f32[:],
                 )
 
-        def copy_and_store(g):
-            cols = slice(g * GROUP_COLS, (g + 1) * GROUP_COLS)
-            nc.scalar.copy(out=out_sb[:, cols], in_=y_turned[g][:].rearrange("r i c -> r (i c)"))
+        def copy_and_store(n):
+            first, tiles = rounds[n]
+            cols = slice(first * C_TILE, (first + tiles) * C_TILE)
+            nc.scalar.copy(out=out_sb[:, cols], in_=y_turned[n][:].rearrange("r i c -> r (i c)"))
             nc.sync.dma_start(out=out_rows[:, cols], in_=out_sb[:, cols])
 
-        for g in range(GROUPS):
-            passes(g)
-        for g in range(RELU_AHEAD):
-            bias_relu(g)
-        for g in range(GROUPS):
-            sum_over_d(g)
-            if g + RELU_AHEAD < GROUPS:
-                bias_relu(g + RELU_AHEAD)
-            turn_back(g)
-        for g in range(GROUPS):
-            copy_and_store(g)
+        for n in range(len(rounds)):
+            passes(n)
+        for n in range(RELU_AHEAD):
+            bias_relu(n)
+        for n in range(len(rounds)):
+            sum_over_d(n)
+            if n + RELU_AHEAD < len(rounds):
+                bias_relu(n + RELU_AHEAD)
+            turn_back(n)
+        for n in range(len(rounds)):
+            copy_and_store(n)

@@ -24,8 +24,11 @@ HALVES = 2
 HALF_TILES = C // (HALVES * C_TILE)
 W_LOADS = 4
 LAST_TILES = 2
-ACC_ROUNDS = 3
+ACC_ROUNDS = 2
+TURNED_BANKS = 4
 RELU_AHEAD = 2
+PASSES_AHEAD = 4
+WARM_MATMULS = 2
 
 FLOPS = 2 * ROWS * F_HID * F_RAW * C
 
@@ -36,7 +39,7 @@ def tile_cin_pb_s_kernel(tc, h2, x0, W3_words, W3_scales, b3, out):
         keep = ctx.enter_context(tc.tile_pool(name="keep", bufs=1))
         work = ctx.enter_context(tc.tile_pool(name="work", bufs=3))
         acc_pool = ctx.enter_context(tc.psum_pool(name="acc", bufs=ACC_ROUNDS))
-        turned_pool = ctx.enter_context(tc.psum_pool(name="turned", bufs=2))
+        turned_pool = ctx.enter_context(tc.psum_pool(name="turned", bufs=TURNED_BANKS))
         ctx.enter_context(tc.manual_schedule())
 
         h2_rows = h2.rearrange("b f d -> b (f d)")
@@ -47,6 +50,17 @@ def tile_cin_pb_s_kernel(tc, h2, x0, W3_words, W3_scales, b3, out):
         nc.sync.dma_start(out=x0_sb[B:P, 0 : F_RAW * D - 1], in_=x0_rows[:, 1:])
         nc.sync.dma_start(out=h2_sb[0:B, :], in_=h2_rows)
         nc.sync.dma_start(out=h2_sb[B:P, 0 : F_HID * D - 1], in_=h2_rows[:, 1:])
+
+        w_words = keep.tile([P, 2 * C], U8, align_bytes=64)
+        words_dram = W3_words[0].rearrange("p (h g n) -> p h g n", h=HALVES, g=W_LOADS)
+        words_sbuf = w_words[:].rearrange("p (h g n) -> p h g n", h=HALVES, g=W_LOADS)
+
+        def load_words(g):
+            nc.sync.dma_start(
+                out=words_sbuf[:, :, g, :].bitcast(I32), in_=words_dram[:, :, g, :].bitcast(I32)
+            )
+
+        load_words(0)
 
         w_scales = keep.tile([P, C], U8, align_bytes=64)
         nc.vector.memset(w_scales[:].bitcast(I32), 0)
@@ -62,13 +76,8 @@ def tile_cin_pb_s_kernel(tc, h2, x0, W3_words, W3_scales, b3, out):
             out=b3_rows[0 : C // C_TILE, :], in_=b3.rearrange("(t c) -> t c", c=C_TILE)
         )
 
-        w_words = keep.tile([P, 2 * C], U8, align_bytes=64)
-        words_dram = W3_words[0].rearrange("p (h g n) -> p h g n", h=HALVES, g=W_LOADS)
-        words_sbuf = w_words[:].rearrange("p (h g n) -> p h g n", h=HALVES, g=W_LOADS)
-        for g in range(W_LOADS):
-            nc.sync.dma_start(
-                out=words_sbuf[:, :, g, :].bitcast(I32), in_=words_dram[:, :, g, :].bitcast(I32)
-            )
+        for g in range(1, W_LOADS):
+            load_words(g)
 
         ident_bf16 = keep.tile([P, P], BF16)
         make_identity(nc, ident_bf16[:])
@@ -89,6 +98,15 @@ def tile_cin_pb_s_kernel(tc, h2, x0, W3_words, W3_scales, b3, out):
         for t in range(PACK):
             nc.tensor.transpose(
                 z_turned[:, t, :], z_rows[:, t, :, :].rearrange("r f s -> r (f s)"), ident_bf16[:]
+            )
+        warm = turned_pool.tile([P, PACK * P], F32, tag="turned")
+        for k in range(WARM_MATMULS):
+            nc.tensor.matmul(
+                out=warm[:],
+                lhsT=ident_bf16[:],
+                rhs=z_rows[:].rearrange("r t f s -> r (t f s)"),
+                start=True,
+                stop=True,
             )
         b3_turned = turned_pool.tile([P, P], BF16, tag="turned")
         nc.tensor.transpose(b3_turned[:], b3_rows[:], ident_bf16[:])
@@ -180,7 +198,7 @@ def tile_cin_pb_s_kernel(tc, h2, x0, W3_words, W3_scales, b3, out):
             nc.scalar.copy(out=out_sb[:, cols], in_=y_turned[n][:].rearrange("r i c -> r (i c)"))
             nc.sync.dma_start(out=out_rows[:, cols], in_=out_sb[:, cols])
 
-        for n in range(len(rounds)):
+        for n in range(PASSES_AHEAD):
             passes(n)
         for n in range(RELU_AHEAD):
             bias_relu(n)
@@ -189,5 +207,8 @@ def tile_cin_pb_s_kernel(tc, h2, x0, W3_words, W3_scales, b3, out):
             if n + RELU_AHEAD < len(rounds):
                 bias_relu(n + RELU_AHEAD)
             turn_back(n)
-        for n in range(len(rounds)):
-            copy_and_store(n)
+            if n + PASSES_AHEAD < len(rounds):
+                passes(n + PASSES_AHEAD)
+            if n >= 1:
+                copy_and_store(n - 1)
+        copy_and_store(len(rounds) - 1)

@@ -28,7 +28,6 @@ ACC_ROUNDS = 2
 TURNED_BANKS = 4
 RELU_AHEAD = 2
 PASSES_AHEAD = 4
-WARM_MATMULS = 2
 
 FLOPS = 2 * ROWS * F_HID * F_RAW * C
 
@@ -98,15 +97,6 @@ def tile_cin_pb_s_kernel(tc, h2, x0, W3_words, W3_scales, b3, out):
         for t in range(PACK):
             nc.tensor.transpose(
                 z_turned[:, t, :], z_rows[:, t, :, :].rearrange("r f s -> r (f s)"), ident_bf16[:]
-            )
-        warm = turned_pool.tile([P, PACK * P], F32, tag="turned")
-        for k in range(WARM_MATMULS):
-            nc.tensor.matmul(
-                out=warm[:],
-                lhsT=ident_bf16[:],
-                rhs=z_rows[:].rearrange("r t f s -> r (t f s)"),
-                start=True,
-                stop=True,
             )
         b3_turned = turned_pool.tile([P, P], BF16, tag="turned")
         nc.tensor.transpose(b3_turned[:], b3_rows[:], ident_bf16[:])

@@ -50,17 +50,6 @@ def tile_cin_pb_s_kernel(tc, h2, x0, W3_words, W3_scales, b3, out):
         nc.sync.dma_start(out=h2_sb[0:B, :], in_=h2_rows)
         nc.sync.dma_start(out=h2_sb[B:P, 0 : F_HID * D - 1], in_=h2_rows[:, 1:])
 
-        w_words = keep.tile([P, 2 * C], U8, align_bytes=64)
-        words_dram = W3_words[0].rearrange("p (h g n) -> p h g n", h=HALVES, g=W_LOADS)
-        words_sbuf = w_words[:].rearrange("p (h g n) -> p h g n", h=HALVES, g=W_LOADS)
-
-        def load_words(g):
-            nc.sync.dma_start(
-                out=words_sbuf[:, :, g, :].bitcast(I32), in_=words_dram[:, :, g, :].bitcast(I32)
-            )
-
-        load_words(0)
-
         w_scales = keep.tile([P, C], U8, align_bytes=64)
         nc.vector.memset(w_scales[:].bitcast(I32), 0)
         for quad in range(4):
@@ -75,8 +64,13 @@ def tile_cin_pb_s_kernel(tc, h2, x0, W3_words, W3_scales, b3, out):
             out=b3_rows[0 : C // C_TILE, :], in_=b3.rearrange("(t c) -> t c", c=C_TILE)
         )
 
-        for g in range(1, W_LOADS):
-            load_words(g)
+        w_words = keep.tile([P, 2 * C], U8, align_bytes=64)
+        words_dram = W3_words[0].rearrange("p (h g n) -> p h g n", h=HALVES, g=W_LOADS)
+        words_sbuf = w_words[:].rearrange("p (h g n) -> p h g n", h=HALVES, g=W_LOADS)
+        for g in range(W_LOADS):
+            nc.sync.dma_start(
+                out=words_sbuf[:, :, g, :].bitcast(I32), in_=words_dram[:, :, g, :].bitcast(I32)
+            )
 
         ident_bf16 = keep.tile([P, P], BF16)
         make_identity(nc, ident_bf16[:])

@@ -28,6 +28,8 @@ ACC_ROUNDS = 2
 TURNED_BANKS = 4
 RELU_AHEAD = 2
 PASSES_AHEAD = 4
+WARM_BEFORE = 8
+WARM_BETWEEN = 3
 
 FLOPS = 2 * ROWS * F_HID * F_RAW * C
 
@@ -40,6 +42,16 @@ def tile_cin_pb_s_kernel(tc, h2, x0, W3_words, W3_scales, b3, out):
         acc_pool = ctx.enter_context(tc.psum_pool(name="acc", bufs=ACC_ROUNDS))
         turned_pool = ctx.enter_context(tc.psum_pool(name="turned", bufs=TURNED_BANKS))
         ctx.enter_context(tc.manual_schedule())
+
+        warm_sb = keep.tile([P, P], F32)
+        nc.vector.memset(warm_sb[:], 0.0)
+        warm_ps = turned_pool.tile([P, P], F32, tag="turned")
+
+        def warm_up(count):
+            for i in range(count):
+                nc.tensor.matmul(out=warm_ps[:], lhsT=warm_sb[:], rhs=warm_sb[:], start=True, stop=True)
+
+        warm_up(WARM_BEFORE)
 
         h2_rows = h2.rearrange("b f d -> b (f d)")
         x0_rows = x0.rearrange("b j d -> b (j d)")
@@ -94,6 +106,7 @@ def tile_cin_pb_s_kernel(tc, h2, x0, W3_words, W3_scales, b3, out):
             )
         b3_turned = turned_pool.tile([P, P], BF16, tag="turned")
         nc.tensor.transpose(b3_turned[:], b3_rows[:], ident_bf16[:])
+        warm_up(WARM_BETWEEN)
 
         z_grouped = keep.tile([P, ROWS, PACK], BF16, align_bytes=64)
         nc.vector.tensor_copy(out=z_grouped[:], in_=z_turned[:].rearrange("p t r -> p r t"))

@@ -15,6 +15,8 @@ ACT = mybir.ActivationFunctionType
 
 P = 128
 PACK = 4
+PAIR = 2
+WORDS = PACK // PAIR
 B, F_HID, F_RAW, D = 64, 64, 8, 2
 C = 4096
 ROWS = D * B
@@ -57,10 +59,8 @@ def tile_cin_pb_s_kernel(tc, h2, x0, W3_words, W3_scales, b3, out):
         x0_rows = x0.rearrange("b j d -> b (j d)")
         x0_sb = keep.tile([P, F_RAW * D], BF16)
         h2_sb = keep.tile([P, F_HID * D], BF16)
-        nc.sync.dma_start(out=x0_sb[0:B, :], in_=x0_rows)
-        nc.sync.dma_start(out=x0_sb[B:P, 0 : F_RAW * D - 1], in_=x0_rows[:, 1:])
         nc.sync.dma_start(out=h2_sb[0:B, :], in_=h2_rows)
-        nc.sync.dma_start(out=h2_sb[B:P, 0 : F_HID * D - 1], in_=h2_rows[:, 1:])
+        nc.sync.dma_start(out=x0_sb[0:B, :], in_=x0_rows)
 
         w_scales = keep.tile([P, C], U8, align_bytes=64)
         nc.vector.memset(w_scales[:].bitcast(I32), 0)
@@ -84,32 +84,41 @@ def tile_cin_pb_s_kernel(tc, h2, x0, W3_words, W3_scales, b3, out):
                 out=words_sbuf[:, :, g, :].bitcast(I32), in_=words_dram[:, :, g, :].bitcast(I32)
             )
 
-        ident_bf16 = keep.tile([P, P], BF16)
-        make_identity(nc, ident_bf16[:])
         ident_f32 = keep.tile([P, P], F32)
         make_identity(nc, ident_f32[:])
+        ident_bf16 = keep.tile([P, P], BF16)
+        make_identity(nc, ident_bf16[:])
 
-        h2_field = h2_sb[:].rearrange("r (f d) -> r f d", d=D)[:, :, 0]
-        x0_field = x0_sb[:].rearrange("r (j d) -> r j d", d=D)[:, :, 0]
-        z_shape = [P, PACK, F_HID, F_RAW // PACK]
-        z_rows = keep.tile(z_shape, BF16)
-        nc.vector.tensor_tensor(
-            out=z_rows[:],
-            in0=h2_field.unsqueeze(1).unsqueeze(3).to_broadcast(z_shape),
-            in1=x0_field.rearrange("r (s t) -> r t s", t=PACK).unsqueeze(2).to_broadcast(z_shape),
-            op=ALU.mult,
-        )
-        z_turned = turned_pool.tile([P, PACK, ROWS], BF16, tag="turned")
-        for t in range(PACK):
-            nc.tensor.transpose(
-                z_turned[:, t, :], z_rows[:, t, :, :].rearrange("r f s -> r (f s)"), ident_bf16[:]
-            )
+        h2_fields = h2_sb[0:B, :].rearrange("b (f d) -> b f d", d=D)
+        x0_fields = x0_sb[0:B, :].rearrange("b (s u e d) -> b u s e d", u=WORDS, e=PAIR, d=D)
+        z_shape = [B, F_HID, F_RAW // PACK, PAIR]
+        z_rows = keep.tile([P, D, WORDS, F_HID, F_RAW // PACK, PAIR], BF16)
+        nc.vector.memset(z_rows[B:P, :, :, :, :, :].rearrange("b d u f s e -> b (d u f s e)").bitcast(F32), 0.0)
+        z_turned = turned_pool.tile([P, D, WORDS, P], F32, tag="turned")
+        for d in range(D):
+            for u in range(WORDS):
+                nc.vector.tensor_tensor(
+                    out=z_rows[0:B, d, u, :, :, :],
+                    in0=h2_fields[:, :, d].unsqueeze(2).unsqueeze(3).to_broadcast(z_shape),
+                    in1=x0_fields[:, u, :, :, d].unsqueeze(1).to_broadcast(z_shape),
+                    op=ALU.mult,
+                )
+        for d in range(D):
+            for u in range(WORDS):
+                nc.tensor.transpose(
+                    z_turned[:, d, u, :],
+                    z_rows[:, d, u, :, :, :].rearrange("r f s e -> r (f s e)").bitcast(F32),
+                    ident_f32[:],
+                )
         b3_turned = turned_pool.tile([P, P], BF16, tag="turned")
         nc.tensor.transpose(b3_turned[:], b3_rows[:], ident_bf16[:])
         warm_up(WARM_BETWEEN)
 
         z_grouped = keep.tile([P, ROWS, PACK], BF16, align_bytes=64)
-        nc.vector.tensor_copy(out=z_grouped[:], in_=z_turned[:].rearrange("p t r -> p r t"))
+        nc.vector.tensor_copy(
+            out=z_grouped[:].rearrange("p r t -> p (r t)").bitcast(F32).rearrange("p (d b u) -> p d b u", d=D, u=WORDS),
+            in_=z_turned[:, :, :, 0:B].rearrange("p d u b -> p d b u"),
+        )
         z_codes = keep.tile([P, ROWS], U32, align_bytes=64)
         z_scales = keep.tile([P, ROWS], U8, align_bytes=64)
         nc.vector.quantize_mx(

@@ -201,8 +201,12 @@ def tile_cin_pb_s_kernel(tc, h2, x0, W3_words, W3_scales, b3, out):
         def copy_and_store(n):
             first, tiles = rounds[n]
             cols = slice(first * C_TILE, (first + tiles) * C_TILE)
-            nc.scalar.copy(out=out_sb[:, cols], in_=y_turned[n][:].rearrange("r i c -> r (i c)"))
-            nc.sync.dma_start(out=out_rows[:, cols], in_=out_sb[:, cols])
+            if n == len(rounds) - 2:
+                nc.vector.tensor_copy(out=out_sb[:, cols], in_=y_turned[n][:].rearrange("r i c -> r (i c)"))
+            else:
+                nc.scalar.copy(out=out_sb[:, cols], in_=y_turned[n][:].rearrange("r i c -> r (i c)"))
+            queue = nc.scalar if n == len(rounds) - 1 else nc.sync
+            queue.dma_start(out=out_rows[:, cols], in_=out_sb[:, cols])
 
         for n in range(PASSES_AHEAD):
             passes(n)

@@ -60,7 +60,7 @@ def tile_cin_pb_s_kernel(tc, h2, x0, W3_words, W3_scales, b3, out):
         x0_sb = keep.tile([P, F_RAW * D], BF16)
         h2_sb = keep.tile([P, F_HID * D], BF16)
         nc.sync.dma_start(out=h2_sb[0:B, :], in_=h2_rows)
-        nc.sync.dma_start(out=x0_sb[0:B, :], in_=x0_rows)
+        nc.scalar.dma_start(out=x0_sb[0:B, :], in_=x0_rows)
 
         w_scales = keep.tile([P, C], U8, align_bytes=64)
         nc.vector.memset(w_scales[:].bitcast(I32), 0)
@@ -94,7 +94,7 @@ def tile_cin_pb_s_kernel(tc, h2, x0, W3_words, W3_scales, b3, out):
         z_shape = [B, F_HID, F_RAW // PACK, PAIR]
         z_rows = keep.tile([P, D, WORDS, F_HID, F_RAW // PACK, PAIR], BF16)
         nc.vector.memset(z_rows[B:P, :, :, :, :, :].rearrange("b d u f s e -> b (d u f s e)").bitcast(F32), 0.0)
-        z_turned = turned_pool.tile([P, D, WORDS, P], F32, tag="turned")
+        z_turned = [turned_pool.tile([P, WORDS, P], F32, name="z_turned%d" % d, tag="turned") for d in range(D)]
         for d in range(D):
             for u in range(WORDS):
                 nc.vector.tensor_tensor(
@@ -106,7 +106,7 @@ def tile_cin_pb_s_kernel(tc, h2, x0, W3_words, W3_scales, b3, out):
         for d in range(D):
             for u in range(WORDS):
                 nc.tensor.transpose(
-                    z_turned[:, d, u, :],
+                    z_turned[d][:, u, :],
                     z_rows[:, d, u, :, :, :].rearrange("r f s e -> r (f s e)").bitcast(F32),
                     ident_f32[:],
                 )
@@ -115,10 +115,9 @@ def tile_cin_pb_s_kernel(tc, h2, x0, W3_words, W3_scales, b3, out):
         warm_up(WARM_BETWEEN)
 
         z_grouped = keep.tile([P, ROWS, PACK], BF16, align_bytes=64)
-        nc.vector.tensor_copy(
-            out=z_grouped[:].rearrange("p r t -> p (r t)").bitcast(F32).rearrange("p (d b u) -> p d b u", d=D, u=WORDS),
-            in_=z_turned[:, :, :, 0:B].rearrange("p d u b -> p d b u"),
-        )
+        z_words = z_grouped[:].rearrange("p r t -> p (r t)").bitcast(F32).rearrange("p (d b u) -> p d b u", d=D, u=WORDS)
+        for d in range(D):
+            nc.vector.tensor_copy(out=z_words[:, d, :, :], in_=z_turned[d][:, :, 0:B].rearrange("p u b -> p b u"))
         z_codes = keep.tile([P, ROWS], U32, align_bytes=64)
         z_scales = keep.tile([P, ROWS], U8, align_bytes=64)
         nc.vector.quantize_mx(

@@ -60,7 +60,7 @@ def tile_cin_pb_s_kernel(tc, h2, x0, W3_words, W3_scales, b3, out):
         x0_sb = keep.tile([P, F_RAW * D], BF16)
         h2_sb = keep.tile([P, F_HID * D], BF16)
         nc.sync.dma_start(out=h2_sb[0:B, :], in_=h2_rows)
-        nc.scalar.dma_start(out=x0_sb[0:B, :], in_=x0_rows)
+        nc.sync.dma_start(out=x0_sb[0:B, :], in_=x0_rows)
 
         w_scales = keep.tile([P, C], U8, align_bytes=64)
         nc.vector.memset(w_scales[:].bitcast(I32), 0)

@@ -30,7 +30,7 @@ ACC_ROUNDS = 2
 TURNED_BANKS = 4
 RELU_AHEAD = 2
 PASSES_AHEAD = 4
-WARM_BEFORE = 8
+WARM_BEFORE = 5
 WARM_BETWEEN = 3
 
 FLOPS = 2 * ROWS * F_HID * F_RAW * C

@@ -76,13 +76,12 @@ def tile_cin_pb_s_kernel(tc, h2, x0, W3_words, W3_scales, b3, out):
             out=b3_rows[0 : C // C_TILE, :], in_=b3.rearrange("(t c) -> t c", c=C_TILE)
         )
 
-        w_words = keep.tile([P, 2 * C], U8, align_bytes=64)
+        load_tiles = HALF_TILES // W_LOADS
         words_dram = W3_words[0].rearrange("p (h g n) -> p h g n", h=HALVES, g=W_LOADS)
-        words_sbuf = w_words[:].rearrange("p (h g n) -> p h g n", h=HALVES, g=W_LOADS)
+        w_words = []
         for g in range(W_LOADS):
-            nc.sync.dma_start(
-                out=words_sbuf[:, :, g, :].bitcast(I32), in_=words_dram[:, :, g, :].bitcast(I32)
-            )
+            w_words.append(keep.tile([P, HALVES, 2 * load_tiles * C_TILE], U8, align_bytes=64, name="w_words%d" % g))
+            nc.sync.dma_start(out=w_words[g][:].bitcast(I32), in_=words_dram[:, :, g, :].bitcast(I32))
 
         ident_f32 = keep.tile([P, P], F32)
         make_identity(nc, ident_f32[:])
@@ -146,9 +145,10 @@ def tile_cin_pb_s_kernel(tc, h2, x0, W3_words, W3_scales, b3, out):
                 acc[n, h] = acc_pool.tile([P, tiles, ROWS], F32, name="acc%d" % h)
                 for i in range(tiles):
                     c0 = (h * HALF_TILES + first + i) * C_TILE
+                    g, in_load = divmod(first + i, load_tiles)
                     nc.tensor.matmul_mx(
                         out=acc[n, h][:, i, :],
-                        lhsT=w_words[:, 2 * c0 : 2 * (c0 + C_TILE)].bitcast(FP4X4),
+                        lhsT=w_words[g][:, h, 2 * in_load * C_TILE : 2 * (in_load + 1) * C_TILE].bitcast(FP4X4),
                         lhsT_scale=w_scales[:, c0 : c0 + C_TILE],
                         rhs=z_codes[:].bitcast(FP8X4),
                         rhs_scale=z_scales[:],

@@ -25,6 +25,9 @@ BANK_TILES = 4
 HALVES = 2
 HALF_TILES = C // (HALVES * C_TILE)
 W_LOADS = 4
+WORD_TILES = HALF_TILES // W_LOADS
+SCALE_LOADS = 2
+SCALE_TILES = HALF_TILES // SCALE_LOADS
 LAST_TILES = 2
 ACC_ROUNDS = 2
 TURNED_BANKS = 4
@@ -46,7 +49,7 @@ def tile_cin_pb_s_kernel(tc, h2, x0, W3_words, W3_scales, b3, out):
         ctx.enter_context(tc.manual_schedule())
 
         warm_sb = keep.tile([P, P], F32)
-        nc.vector.memset(warm_sb[:], 0.0)
+        nc.gpsimd.memset(warm_sb[:], 0.0)
         warm_ps = turned_pool.tile([P, P], F32, tag="turned")
 
         def warm_up(count):
@@ -62,13 +65,26 @@ def tile_cin_pb_s_kernel(tc, h2, x0, W3_words, W3_scales, b3, out):
         nc.sync.dma_start(out=h2_sb[0:B, :], in_=h2_rows)
         nc.sync.dma_start(out=x0_sb[0:B, :], in_=x0_rows)
 
-        w_scales = keep.tile([P, C], U8, align_bytes=64)
-        nc.vector.memset(w_scales[:].bitcast(I32), 0)
-        for quad in range(4):
-            nc.sync.dma_start(
-                out=w_scales[32 * quad : 32 * quad + 4, :].bitcast(I32),
-                in_=W3_scales[0, 4 * quad : 4 * quad + 4, :].bitcast(I32),
-            )
+        words_dram = W3_words[0].rearrange("p (h g n) -> p h g n", h=HALVES, g=W_LOADS)
+        w_words = []
+
+        def load_words():
+            g = len(w_words)
+            w_words.append(keep.tile([P, HALVES, 2 * WORD_TILES * C_TILE], U8, align_bytes=64, name="w_words%d" % g))
+            nc.sync.dma_start(out=w_words[g][:].bitcast(I32), in_=words_dram[:, :, g, :].bitcast(I32))
+
+        scales_dram = W3_scales[0].rearrange("q (h g n) -> q h g n", h=HALVES, g=SCALE_LOADS)
+        w_scales = []
+        for g in range(SCALE_LOADS):
+            w_scales.append(keep.tile([P, HALVES, SCALE_TILES * C_TILE], U8, align_bytes=64, name="w_scales%d" % g))
+            nc.vector.memset(w_scales[g][:].rearrange("p h n -> p (h n)").bitcast(I32), 0)
+
+        def load_scales(g):
+            for quad in range(4):
+                nc.sync.dma_start(
+                    out=w_scales[g][32 * quad : 32 * quad + 4, :, :].bitcast(I32),
+                    in_=scales_dram[4 * quad : 4 * quad + 4, :, g, :].bitcast(I32),
+                )
 
         b3_rows = keep.tile([P, P], BF16)
         nc.gpsimd.memset(b3_rows[:], 0.0)
@@ -76,12 +92,12 @@ def tile_cin_pb_s_kernel(tc, h2, x0, W3_words, W3_scales, b3, out):
             out=b3_rows[0 : C // C_TILE, :], in_=b3.rearrange("(t c) -> t c", c=C_TILE)
         )
 
-        load_tiles = HALF_TILES // W_LOADS
-        words_dram = W3_words[0].rearrange("p (h g n) -> p h g n", h=HALVES, g=W_LOADS)
-        w_words = []
-        for g in range(W_LOADS):
-            w_words.append(keep.tile([P, HALVES, 2 * load_tiles * C_TILE], U8, align_bytes=64, name="w_words%d" % g))
-            nc.sync.dma_start(out=w_words[g][:].bitcast(I32), in_=words_dram[:, :, g, :].bitcast(I32))
+        load_words()
+        load_scales(0)
+        load_words()
+        load_scales(1)
+        load_words()
+        load_words()
 
         ident_f32 = keep.tile([P, P], F32)
         make_identity(nc, ident_f32[:])
@@ -144,12 +160,12 @@ def tile_cin_pb_s_kernel(tc, h2, x0, W3_words, W3_scales, b3, out):
             for h in range(HALVES):
                 acc[n, h] = acc_pool.tile([P, tiles, ROWS], F32, name="acc%d" % h)
                 for i in range(tiles):
-                    c0 = (h * HALF_TILES + first + i) * C_TILE
-                    g, in_load = divmod(first + i, load_tiles)
+                    g, in_load = divmod(first + i, WORD_TILES)
+                    s, in_set = divmod(first + i, SCALE_TILES)
                     nc.tensor.matmul_mx(
                         out=acc[n, h][:, i, :],
                         lhsT=w_words[g][:, h, 2 * in_load * C_TILE : 2 * (in_load + 1) * C_TILE].bitcast(FP4X4),
-                        lhsT_scale=w_scales[:, c0 : c0 + C_TILE],
+                        lhsT_scale=w_scales[s][:, h, in_set * C_TILE : (in_set + 1) * C_TILE],
                         rhs=z_codes[:].bitcast(FP8X4),
                         rhs_scale=z_scales[:],
                         start=True,

from contextlib import ExitStack

import concourse.mybir as mybir
from concourse.masks import make_identity

BF16 = mybir.dt.bfloat16
F32 = mybir.dt.float32
I32 = mybir.dt.int32
U8 = mybir.dt.uint8
U32 = mybir.dt.uint32
FP8X4 = mybir.dt.float8_e4m3fn_x4
FP4X4 = mybir.dt.float4_e2m1fn_x4
ALU = mybir.AluOpType
ACT = mybir.ActivationFunctionType

P = 128
PACK = 4
PAIR = 2
WORDS = PACK // PAIR
B, F_HID, F_RAW, D = 64, 64, 8, 2
C = 4096
ROWS = D * B
C_TILE = 128
BANK_TILES = 4
HALVES = 2
HALF_TILES = C // (HALVES * C_TILE)
W_LOADS = 4
WORD_TILES = HALF_TILES // W_LOADS
SCALE_LOADS = 2
SCALE_TILES = HALF_TILES // SCALE_LOADS
LAST_TILES = 2
ACC_ROUNDS = 2
TURNED_BANKS = 4
RELU_AHEAD = 2
PASSES_AHEAD = 4
WARM_BEFORE = 5
WARM_BETWEEN = 3

FLOPS = 2 * ROWS * F_HID * F_RAW * C


def tile_cin_pb_s_kernel(tc, h2, x0, W3_words, W3_scales, b3, out):
    nc = tc.nc
    with ExitStack() as ctx:
        keep = ctx.enter_context(tc.tile_pool(name="keep", bufs=1))
        work = ctx.enter_context(tc.tile_pool(name="work", bufs=3))
        acc_pool = ctx.enter_context(tc.psum_pool(name="acc", bufs=ACC_ROUNDS))
        turned_pool = ctx.enter_context(tc.psum_pool(name="turned", bufs=TURNED_BANKS))
        ctx.enter_context(tc.manual_schedule())

        warm_sb = keep.tile([P, P], F32)
        nc.gpsimd.memset(warm_sb[:], 0.0)
        warm_ps = turned_pool.tile([P, P], F32, tag="turned")

        def warm_up(count):
            for i in range(count):
                nc.tensor.matmul(out=warm_ps[:], lhsT=warm_sb[:], rhs=warm_sb[:], start=True, stop=True)

        warm_up(WARM_BEFORE)

        h2_rows = h2.rearrange("b f d -> b (f d)")
        x0_rows = x0.rearrange("b j d -> b (j d)")
        x0_sb = keep.tile([P, F_RAW * D], BF16)
        h2_sb = keep.tile([P, F_HID * D], BF16)
        nc.sync.dma_start(out=h2_sb[0:B, :], in_=h2_rows)
        nc.sync.dma_start(out=x0_sb[0:B, :], in_=x0_rows)

        words_dram = W3_words[0].rearrange("p (h g n) -> p h g n", h=HALVES, g=W_LOADS)
        w_words = []

        def load_words():
            g = len(w_words)
            w_words.append(keep.tile([P, HALVES, 2 * WORD_TILES * C_TILE], U8, align_bytes=64, name="w_words%d" % g))
            nc.sync.dma_start(out=w_words[g][:].bitcast(I32), in_=words_dram[:, :, g, :].bitcast(I32))

        scales_dram = W3_scales[0].rearrange("q (h g n) -> q h g n", h=HALVES, g=SCALE_LOADS)
        w_scales = []
        for g in range(SCALE_LOADS):
            w_scales.append(keep.tile([P, HALVES, SCALE_TILES * C_TILE], U8, align_bytes=64, name="w_scales%d" % g))
            nc.vector.memset(w_scales[g][:].rearrange("p h n -> p (h n)").bitcast(I32), 0)

        def load_scales(g):
            for quad in range(4):
                nc.sync.dma_start(
                    out=w_scales[g][32 * quad : 32 * quad + 4, :, :].bitcast(I32),
                    in_=scales_dram[4 * quad : 4 * quad + 4, :, g, :].bitcast(I32),
                )

        b3_rows = keep.tile([P, P], BF16)
        nc.gpsimd.memset(b3_rows[:], 0.0)
        nc.scalar.dma_start(
            out=b3_rows[0 : C // C_TILE, :], in_=b3.rearrange("(t c) -> t c", c=C_TILE)
        )

        load_words()
        load_scales(0)
        load_words()
        load_scales(1)
        load_words()
        load_words()

        ident_f32 = keep.tile([P, P], F32)
        make_identity(nc, ident_f32[:])
        ident_bf16 = keep.tile([P, P], BF16)
        make_identity(nc, ident_bf16[:])

        h2_fields = h2_sb[0:B, :].rearrange("b (f d) -> b f d", d=D)
        x0_fields = x0_sb[0:B, :].rearrange("b (s u e d) -> b u s e d", u=WORDS, e=PAIR, d=D)
        z_shape = [B, F_HID, F_RAW // PACK, PAIR]
        z_rows = keep.tile([P, D, WORDS, F_HID, F_RAW // PACK, PAIR], BF16)
        nc.vector.memset(z_rows[B:P, :, :, :, :, :].rearrange("b d u f s e -> b (d u f s e)").bitcast(F32), 0.0)
        z_turned = [turned_pool.tile([P, WORDS, P], F32, name="z_turned%d" % d, tag="turned") for d in range(D)]
        for d in range(D):
            for u in range(WORDS):
                nc.vector.tensor_tensor(
                    out=z_rows[0:B, d, u, :, :, :],
                    in0=h2_fields[:, :, d].unsqueeze(2).unsqueeze(3).to_broadcast(z_shape),
                    in1=x0_fields[:, u, :, :, d].unsqueeze(1).to_broadcast(z_shape),
                    op=ALU.mult,
                )
        for d in range(D):
            for u in range(WORDS):
                nc.tensor.transpose(
                    z_turned[d][:, u, :],
                    z_rows[:, d, u, :, :, :].rearrange("r f s e -> r (f s e)").bitcast(F32),
                    ident_f32[:],
                )
        b3_turned = turned_pool.tile([P, P], BF16, tag="turned")
        nc.tensor.transpose(b3_turned[:], b3_rows[:], ident_bf16[:])
        warm_up(WARM_BETWEEN)

        z_grouped = keep.tile([P, ROWS, PACK], BF16, align_bytes=64)
        z_words = z_grouped[:].rearrange("p r t -> p (r t)").bitcast(F32).rearrange("p (d b u) -> p d b u", d=D, u=WORDS)
        for d in range(D):
            nc.vector.tensor_copy(out=z_words[:, d, :, :], in_=z_turned[d][:, :, 0:B].rearrange("p u b -> p b u"))
        z_codes = keep.tile([P, ROWS], U32, align_bytes=64)
        z_scales = keep.tile([P, ROWS], U8, align_bytes=64)
        nc.vector.quantize_mx(
            out=z_codes[:].bitcast(FP8X4),
            scales=z_scales[:],
            in_=z_grouped[:].rearrange("p r t -> p (r t)"),
        )

        bias = keep.tile([P, C // C_TILE], F32)
        nc.scalar.copy(out=bias[:], in_=b3_turned[:, 0 : C // C_TILE])

        out_rows = out.rearrange("b (h n) -> (b h) n", h=HALVES)
        out_sb = keep.tile([P, C // HALVES], F32)

        rounds = [(first, BANK_TILES) for first in range(0, HALF_TILES - BANK_TILES, BANK_TILES)]
        rounds += [(first, LAST_TILES) for first in range(HALF_TILES - BANK_TILES, HALF_TILES, LAST_TILES)]

        acc = {}
        y = {}
        y_sum = {}
        y_turned = {}

        def passes(n):
            first, tiles = rounds[n]
            for h in range(HALVES):
                acc[n, h] = acc_pool.tile([P, tiles, ROWS], F32, name="acc%d" % h)
                for i in range(tiles):
                    g, in_load = divmod(first + i, WORD_TILES)
                    s, in_set = divmod(first + i, SCALE_TILES)
                    nc.tensor.matmul_mx(
                        out=acc[n, h][:, i, :],
                        lhsT=w_words[g][:, h, 2 * in_load * C_TILE : 2 * (in_load + 1) * C_TILE].bitcast(FP4X4),
                        lhsT_scale=w_scales[s][:, h, in_set * C_TILE : (in_set + 1) * C_TILE],
                        rhs=z_codes[:].bitcast(FP8X4),
                        rhs_scale=z_scales[:],
                        start=True,
                        stop=True,
                    )

        def bias_relu(n):
            first, tiles = rounds[n]
            y[n] = work.tile([P, HALVES, tiles, ROWS], F32, name="y")
            for i in range(tiles):
                t_left = first + i
                nc.vector.tensor_scalar(
                    out=y[n][:, 0, i, :],
                    in0=acc[n, 0][:, i, :],
                    scalar1=bias[:, t_left : t_left + 1],
                    scalar2=0.0,
                    op0=ALU.add,
                    op1=ALU.max,
                )
            for i in range(tiles):
                t_right = HALF_TILES + first + i
                nc.scalar.activation(
                    out=y[n][:, 1, i, :],
                    in_=acc[n, 1][:, i, :],
                    func=ACT.Relu,
                    bias=bias[:, t_right : t_right + 1],
                    scale=1.0,
                )

        def sum_over_d(n):
            tiles = rounds[n][1]
            y_by_d = y[n][:].rearrange("c h i (d b) -> c d i b h", d=D)
            y_sum[n] = work.tile([P, tiles, B, HALVES], F32, name="y_sum")
            nc.vector.tensor_tensor(
                out=y_sum[n][:], in0=y_by_d[:, 0, :, :, :], in1=y_by_d[:, 1, :, :, :], op=ALU.add
            )

        def turn_back(n):
            tiles = rounds[n][1]
            y_turned[n] = turned_pool.tile([P, tiles, C_TILE], F32, name="y_turned", tag="turned")
            for i in range(tiles):
                nc.tensor.transpose(
                    y_turned[n][:, i, :],
                    y_sum[n][:, i, :, :].rearrange("c b h -> c (b h)"),
                    ident_f32[:],
                )

        def copy_and_store(n):
            first, tiles = rounds[n]
            cols = slice(first * C_TILE, (first + tiles) * C_TILE)
            if n == len(rounds) - 2:
                nc.vector.tensor_copy(out=out_sb[:, cols], in_=y_turned[n][:].rearrange("r i c -> r (i c)"))
            else:
                nc.scalar.copy(out=out_sb[:, cols], in_=y_turned[n][:].rearrange("r i c -> r (i c)"))
            queue = nc.scalar if n == len(rounds) - 1 else nc.sync
            queue.dma_start(out=out_rows[:, cols], in_=out_sb[:, cols])

        for n in range(PASSES_AHEAD):
            passes(n)
        for n in range(RELU_AHEAD):
            bias_relu(n)
        for n in range(len(rounds)):
            sum_over_d(n)
            if n + RELU_AHEAD < len(rounds):
                bias_relu(n + RELU_AHEAD)
            turn_back(n)
            if n + PASSES_AHEAD < len(rounds):
                passes(n + PASSES_AHEAD)
            if n >= 1:
                copy_and_store(n - 1)
        copy_and_store(len(rounds) - 1)
